import numpy as np
import ml_dtypes


def mxq(x, axis, fmt="e4m3"):
    dtype, down = {"e4m3": (ml_dtypes.float8_e4m3fn, 7), "e5m2": (ml_dtypes.float8_e5m2, 14)}[fmt]
    v = np.moveaxis(np.asarray(x, np.float32).astype(ml_dtypes.bfloat16).astype(np.float64), axis, -1)
    blocks = v.reshape(v.shape[:-1] + (-1, 32))
    amax = np.abs(blocks).max(-1, keepdims=True)
    byte = np.maximum(np.where(amax > 0, np.frexp(amax)[1] - 1 + 127, 0) - down, 1)
    scale = np.exp2(byte - 127.0)
    codes = (blocks / scale).astype(np.float32).astype(dtype).astype(np.float64)
    return np.moveaxis((codes * scale).reshape(v.shape), -1, axis)


WIDE = False


def mx_kscale(k):
    if not WIDE:
        return np.ones(k)
    levels = np.array([10, -10, 5, -5, 0])
    if k % 512:
        return np.exp2(np.random.permutation(np.resize(levels, k // 32))).repeat(32)
    a = np.empty((k // 512, 16))
    for p in range(k // 512):
        a[p, :8] = np.random.permutation(np.resize(levels, 8))
        for g in range(8):
            far = levels[np.abs(levels - a[p, g]) >= 10]
            a[p, g + 8] = far[np.random.randint(len(far))]
    return np.exp2(a.ravel()).repeat(32)


BF16 = ml_dtypes.bfloat16


def bf(x):
    return np.asarray(x, np.float32).astype(BF16)


def f64(x):
    return np.asarray(x).astype(np.float64)


N, D, H, E = 1024, 512, 2048, 8

CLAMP_MAX = float(np.log(100.0))


def draw0():
    s, t = mx_kscale(D), mx_kscale(H)
    return {"x": bf(np.random.standard_normal((N, D)) * s),
            "W1": bf(np.random.standard_normal((E, D, H)) / np.sqrt(D) / s[:, None] * t),
            "b1": bf(np.random.standard_normal((E, H)) * 0.1 * t),
            "W2": bf(np.random.standard_normal((E, H, D)) / np.sqrt(H) / t[:, None]),
            "b2": bf(np.random.standard_normal((E, D)) * 0.1),
            "temperature": bf(np.log(2.0) + 0.1 * np.random.standard_normal((1,)))}


def core(x, W1, b1, W2, b2, temperature):
    xe = f64(x).reshape(E, N // E, D)
    h = np.maximum((mxq(xe, 2, "e4m3") @ mxq(f64(W1), 1, "e4m3")) + f64(b1)[:, None, :], 0.0)
    y = (mxq(h, 2, "e4m3") @ mxq(f64(W2), 1, "e4m3")) + f64(b2)[:, None, :]
    logit_scale = np.exp(np.minimum(f64(temperature), CLAMP_MAX))
    return y.reshape(N, D) * logit_scale


def e4m3fn_bytes(y):
    return np.clip(np.asarray(y, np.float64), -448.0, 448.0).astype(np.float32).astype(ml_dtypes.float8_e4m3fn).view(np.uint8)


def e4m3fn_values(b):
    return np.asarray(b, np.uint8).view(ml_dtypes.float8_e4m3fn).astype(np.float64)


def setup_inputs():
    d = draw0()
    x0 = np.asarray(d['W2']).astype(np.float64)
    s = (np.max(np.abs(x0), axis=(0, 2), keepdims=True) / 448.0).astype(np.float32)
    out = {}
    for k, v in d.items():
        if k == 'W2':
            out['W2_bytes'] = e4m3fn_bytes(x0 / s.astype(np.float64))
            out['W2_scale'] = s
        else:
            out[k] = v
    return out


def reference(x, W1, b1, W2_bytes, W2_scale, b2, temperature):
    return core(x, W1, b1, e4m3fn_values(W2_bytes) * W2_scale.astype(np.float64), b2, temperature)

@@ -1,0 +1,293 @@
+import math
+from contextlib import ExitStack
+
+import concourse.mybir as mybir
+from concourse.masks import make_identity
+
+F32 = mybir.dt.float32
+BF16 = mybir.dt.bfloat16
+U32 = mybir.dt.uint32
+U8 = mybir.dt.uint8
+FP8 = mybir.dt.float8_e4m3fn
+FP8X4 = mybir.dt.float8_e4m3fn_x4
+ALU = mybir.AluOpType
+ACT = mybir.ActivationFunctionType
+
+N, D, H, E = 1024, 512, 2048, 8
+P = 128
+TOK = N // E
+G = H // 512
+CLAMP_MAX = float(math.log(100.0))
+FLOPS = 2 * N * D * H * 2
+
+
+def tile_moelayer_kernel(tc, x, W1, b1, W2_bytes, W2_scale, b2, temperature, out):
+    nc = tc.nc
+    load = {"v": 0.0, "s": 0.0}
+
+    def use(engine, ns):
+        load[engine] += ns
+
+    def pick(v_ns, s_ns):
+        if load["v"] + v_ns <= load["s"] + s_ns:
+            load["v"] += v_ns
+            return "v"
+        load["s"] += s_ns
+        return "s"
+
+    def copy(engine, dst, src):
+        if engine == "v":
+            nc.vector.tensor_copy(out=dst, in_=src)
+        else:
+            nc.scalar.copy(out=dst, in_=src)
+
+    with ExitStack() as ctx:
+        const = ctx.enter_context(tc.tile_pool(name="const", bufs=1))
+        w1_pool = ctx.enter_context(tc.tile_pool(name="w1_pool", bufs=4))
+        byte_pool = ctx.enter_context(tc.tile_pool(name="byte_pool", bufs=3))
+        work = ctx.enter_context(tc.tile_pool(name="work", bufs=3))
+        codes = ctx.enter_context(tc.tile_pool(name="codes", bufs=4))
+        w2_codes = ctx.enter_context(tc.tile_pool(name="w2_codes", bufs=10))
+        h_pool = ctx.enter_context(tc.tile_pool(name="h_pool", bufs=4))
+        hq_pool = ctx.enter_context(tc.tile_pool(name="hq_pool", bufs=8))
+        out_pool = ctx.enter_context(tc.tile_pool(name="out_pool", bufs=3))
+        ps_t = ctx.enter_context(tc.psum_pool(name="ps_t", bufs=2))
+        ps_h = ctx.enter_context(tc.psum_pool(name="ps_h", bufs=3))
+        ps_y = ctx.enter_context(tc.psum_pool(name="ps_y", bufs=2))
+
+        w1_raw = {}
+        w2_raw = {}
+
+        def load_w1(e, half):
+            raw = w1_pool.tile([P, 4, 1024], BF16, name="raw", align_bytes=64)
+            src = W1[e].rearrange("(p j) n -> p j n", j=4)
+            if e == 0 and half == 0:
+                for q in range(2):
+                    nc.sync.dma_start(out=raw[:, :, q * 512:(q + 1) * 512], in_=src[:, :, q * 512:(q + 1) * 512])
+            else:
+                nc.sync.dma_start(out=raw[:], in_=src[:, :, half * 1024:(half + 1) * 1024])
+            w1_raw[e, half] = raw
+
+        def load_w2(e):
+            wb = byte_pool.tile([P, G, 2048], U8, name="wb", align_bytes=64)
+            src = W2_bytes[e].rearrange("(g p s) n -> p g (s n)", p=P, s=4)
+            nc.sync.dma_start(out=wb[:], in_=src)
+            w2_raw[e] = wb
+
+        load_w1(0, 0)
+        b1_rows = const.tile([32, 512], BF16, name="b1_rows", align_bytes=64)
+        nc.sync.dma_start(out=b1_rows[:], in_=b1.rearrange("e (g c) -> (e g) c", c=512))
+        rows = const.tile([P, 512], F32, name="rows", align_bytes=64)
+        nc.vector.memset(rows[:], 0.0)
+        nc.sync.dma_start(out=rows[32:36, :], in_=W2_scale.rearrange("o (g c) z -> (o g) (c z)", c=512))
+        temp = const.tile([P, 1], BF16, name="temp", align_bytes=64)
+        nc.sync.dma_start(out=temp[:], in_=temperature.partition_broadcast(P))
+        x_all = const.tile([P, E, D], BF16, name="x_all", align_bytes=64)
+        x_src = x.rearrange("(e p) d -> p e d", p=P)
+        nc.sync.dma_start(out=x_all[:, 0:4, :], in_=x_src[:, 0:4, :])
+        load_w2(0)
+        load_w1(0, 1)
+        nc.sync.dma_start(out=x_all[:, 4:8, :], in_=x_src[:, 4:8, :])
+
+        ident = const.tile([P, P], F32, name="ident", align_bytes=64)
+        make_identity(nc, ident[:])
+
+        nc.vector.tensor_copy(out=rows[0:32, :], in_=b1_rows[:])
+        rows_s = const.tile([P, 4, P], F32, name="rows_s", align_bytes=64)
+        nc.vector.tensor_copy(out=rows_s[:], in_=rows[:].rearrange("r (m s) -> r s m", s=4))
+        col_ps = ps_t.tile([P, 4, P], F32, name="tp")
+        for s in range(4):
+            nc.tensor.transpose(col_ps[:, s, :], rows_s[:, s, :], ident[:])
+        cols = const.tile([P, 36, 4], F32, name="cols", align_bytes=64)
+        nc.vector.tensor_copy(out=cols[:], in_=col_ps[:, :, 0:36].rearrange("p s r -> p r s"))
+
+        clamped = const.tile([P, 1], F32, name="clamped", align_bytes=64)
+        nc.vector.tensor_scalar_min(clamped[:], temp[:], CLAMP_MAX)
+        gain = const.tile([P, 1], F32, name="gain", align_bytes=64)
+        nc.scalar.activation(out=gain[:], in_=clamped[:], func=ACT.Exp)
+
+        xq = const.tile([P, E, TOK], U32, name="xq", align_bytes=64)
+        xs = const.tile([P, E, TOK], U8, name="xs", align_bytes=64)
+
+        def x_pair(k):
+            tp = ps_t.tile([P, 4, P], F32, name="tp")
+            for i in range(2):
+                words = x_all[:, 2 * k + i, :].bitcast(F32)
+                for u in range(2):
+                    nc.tensor.transpose(tp[:, 2 * i + u, :], words[:, u:256:2], ident[:])
+            xg = work.tile([P, 2, TOK, 4], BF16, name="xg", align_bytes=64)
+            for i in range(2):
+                nc.vector.tensor_copy(
+                    out=xg[:, i, :, :].bitcast(F32),
+                    in_=tp[:, 2 * i:2 * i + 2, :].rearrange("p u r -> p r u"),
+                )
+            nc.vector.quantize_mx(
+                out=xq[:, 2 * k:2 * k + 2, :].rearrange("p e r -> p (e r)").bitcast(FP8X4),
+                scales=xs[:, 2 * k:2 * k + 2, :].rearrange("p e r -> p (e r)"),
+                in_=xg[:].rearrange("p e r t -> p (e r t)"),
+            )
+            use("v", 2 * 230 + 240)
+
+        b2_all = const.tile([P, E * D], BF16, name="b2_all", align_bytes=64)
+
+        w1_grp, w1_codes, w2_pl, w2_grp, w2_cod, h_ps, h_pl, h_grp, h_cod, y_ps, b2g = ({} for i in range(11))
+
+        def w1_interleave(e, g):
+            raw = w1_raw[e, g // 2]
+            grp = work.tile([P, 4, P, 4], BF16, name="w1g", align_bytes=64)
+            src = raw[:, :, (g % 2) * 512:(g % 2 + 1) * 512].rearrange("p j (m s) -> p m s j", s=4)
+            copy(pick(1080, 2050), grp[:].rearrange("p s m j -> p m s j"), src)
+            w1_grp[e, g] = grp
+
+        def w1_quantise(e, g):
+            q = codes.tile([P, 512], U32, name="w1q", align_bytes=64)
+            sc = codes.tile([P, 512], U8, name="w1s", align_bytes=64)
+            nc.vector.quantize_mx(
+                out=q[:].bitcast(FP8X4), scales=sc[:],
+                in_=w1_grp[e, g][:].rearrange("p s m j -> p (s m j)"),
+            )
+            use("v", 480)
+            w1_codes[e, g] = (q, sc)
+
+        def w2_widen(e, g):
+            plane = work.tile([P, 4, 512], BF16, name="w2p", align_bytes=64)
+            for s in range(4):
+                src = w2_raw[e][:, g, s * 512:(s + 1) * 512].bitcast(FP8)
+                col = cols[:, 32 + g, s:s + 1]
+                if pick(230, 450) == "v":
+                    nc.vector.tensor_scalar(out=plane[:, s, :], in0=src, scalar1=col, scalar2=None, op0=ALU.mult)
+                else:
+                    nc.scalar.activation(out=plane[:, s, :], in_=src, func=ACT.Copy, scale=col)
+            w2_pl[e, g] = plane
+
+        def w2_interleave(e, g):
+            grp = work.tile([P, 512, 4], BF16, name="w2g", align_bytes=64)
+            copy(
+                pick(1080, 2050),
+                grp[:].rearrange("p (c i) s -> p c s i", i=4),
+                w2_pl[e, g][:].rearrange("p s (c i) -> p c s i", i=4),
+            )
+            w2_grp[e, g] = grp
+
+        def w2_quantise(e, g):
+            q = w2_codes.tile([P, 512], U32, name="w2q", align_bytes=64)
+            sc = w2_codes.tile([P, 512], U8, name="w2s", align_bytes=64)
+            nc.vector.quantize_mx(
+                out=q[:].bitcast(FP8X4), scales=sc[:], in_=w2_grp[e, g][:].rearrange("p n s -> p (n s)")
+            )
+            use("v", 480)
+            w2_cod[e, g] = (q, sc)
+
+        def mm1(e, g):
+            q, sc = w1_codes[e, g]
+            ph = ps_h.tile([P, 4, TOK], F32, name="ph")
+            for s in range(4):
+                nc.tensor.matmul_mx(
+                    out=ph[:, s, :],
+                    lhsT=q[:, s * P:(s + 1) * P].bitcast(FP8X4), lhsT_scale=sc[:, s * P:(s + 1) * P],
+                    rhs=xq[:, e, :].bitcast(FP8X4), rhs_scale=xs[:, e, :],
+                    start=True, stop=True,
+                )
+            h_ps[e, g] = ph
+
+        def h_relu(e, g):
+            ph = h_ps[e, g]
+            plane = h_pool.tile([P, 4, TOK], BF16, name="hp", align_bytes=64)
+            for s in range(4):
+                nc.scalar.activation(
+                    out=plane[:, s, :], in_=ph[:, s, :], func=ACT.Relu, bias=cols[:, 4 * e + g, s:s + 1]
+                )
+            use("s", 600)
+            h_pl[e, g] = plane
+
+        def h_interleave(e, g):
+            grp = h_pool.tile([P, TOK, 4], BF16, name="hg", align_bytes=64)
+            copy(
+                pick(285, 530),
+                grp[:].rearrange("p (c i) s -> p c s i", i=4),
+                h_pl[e, g][:].rearrange("p s (c i) -> p c s i", i=4),
+            )
+            h_grp[e, g] = grp
+
+        def h_quantise(e, g):
+            q = hq_pool.tile([P, TOK], U32, name="hq", align_bytes=64)
+            sc = hq_pool.tile([P, TOK], U8, name="hs", align_bytes=64)
+            nc.vector.quantize_mx(
+                out=q[:].bitcast(FP8X4), scales=sc[:], in_=h_grp[e, g][:].rearrange("p n s -> p (n s)")
+            )
+            use("v", 140)
+            h_cod[e, g] = (q, sc)
+
+        def mm2(e):
+            py = ps_y.tile([TOK, D], F32, name="py")
+            for g in range(G):
+                hq, hs = h_cod[e, g]
+                wq, ws = w2_cod[e, g]
+                nc.tensor.matmul_mx(
+                    out=py[:], lhsT=hq[:].bitcast(FP8X4), lhsT_scale=hs[:],
+                    rhs=wq[:].bitcast(FP8X4), rhs_scale=ws[:],
+                    start=(g == 0), stop=(g == G - 1),
+                )
+            y_ps[e] = py
+
+        def bias2(e):
+            bg = out_pool.tile([P, D], F32, name="bg", align_bytes=64)
+            src = b2_all[:, e * D:(e + 1) * D]
+            if pick(240, 450) == "v":
+                nc.vector.tensor_scalar(out=bg[:], in0=src, scalar1=gain[:], scalar2=None, op0=ALU.mult)
+            else:
+                nc.scalar.activation(out=bg[:], in_=src, func=ACT.Copy, scale=gain[:])
+            b2g[e] = bg
+
+        def store(e):
+            y = out_pool.tile([TOK, D], F32, name="y", align_bytes=64)
+            nc.vector.scalar_tensor_tensor(
+                out=y[:], in0=y_ps[e][:], scalar=gain[:], in1=b2g[e][:], op0=ALU.mult, op1=ALU.add
+            )
+            use("v", 450)
+            nc.sync.dma_start(out=out[e * TOK:(e + 1) * TOK, :], in_=y[:])
+
+        units = [(e, g) for e in range(E) for g in range(G)]
+        n_units = len(units)
+
+        def at(i):
+            return units[i] if 0 <= i < n_units else None
+
+        for i in range(n_units + 8):
+            u = at(i)
+            if u is not None:
+                e, g = u
+                if g == 0 and e + 1 < E:
+                    load_w1(e + 1, 0)
+                    load_w2(e + 1)
+                    load_w1(e + 1, 1)
+                if e == 0 and g == 2:
+                    nc.sync.dma_start(out=b2_all[:], in_=b2.rearrange("e d -> (e d)").partition_broadcast(P))
+                w1_interleave(e, g)
+                if i < 4:
+                    x_pair(i)
+                w2_widen(e, g)
+            u = at(i - 1)
+            if u is not None:
+                w1_quantise(*u)
+                w2_interleave(*u)
+            u = at(i - 2)
+            if u is not None:
+                w2_quantise(*u)
+                mm1(*u)
+            u = at(i - 3)
+            if u is not None:
+                h_relu(*u)
+            u = at(i - 4)
+            if u is not None:
+                h_interleave(*u)
+            u = at(i - 5)
+            if u is not None:
+                h_quantise(*u)
+                if u[1] == 2:
+                    bias2(u[0])
+                if u[1] == G - 1:
+                    mm2(u[0])
+            u = at(i - 6)
+            if u is not None and u[1] == G - 1:
+                store(u[0])

@@ -17,23 +17,23 @@ N, D, H, E = 1024, 512, 2048, 8
 P = 128
 TOK = N // E
 G = H // 512
+FILL = 4
+PER_TICK = (2, 2, 2, 2, 2, 2, 2, 2, 1, 1, 1, 1)
+D_SPLIT = 84
+W_SPLIT = 82
+H_SPLIT = 0
 CLAMP_MAX = float(math.log(100.0))
 FLOPS = 2 * N * D * H * 2
 
 
 def tile_moelayer_kernel(tc, x, W1, b1, W2_bytes, W2_scale, b2, temperature, out):
     nc = tc.nc
-    load = {"v": 0.0, "s": 0.0}
 
-    def use(engine, ns):
-        load[engine] += ns
-
-    def pick(v_ns, s_ns):
-        if load["v"] + v_ns <= load["s"] + s_ns:
-            load["v"] += v_ns
-            return "v"
-        load["s"] += s_ns
-        return "s"
+    def split_copy(dst, src, s_part):
+        if s_part > 0:
+            nc.scalar.copy(out=dst[:, 0:s_part], in_=src[:, 0:s_part])
+        if s_part < dst.shape[1]:
+            nc.vector.tensor_copy(out=dst[:, s_part:dst.shape[1]], in_=src[:, s_part:dst.shape[1]])
 
     def copy(engine, dst, src):
         if engine == "v":
@@ -42,58 +42,76 @@ def tile_moelayer_kernel(tc, x, W1, b1, W2_bytes, W2_scale, b2, temperature, out
             nc.scalar.copy(out=dst, in_=src)
 
     with ExitStack() as ctx:
+        ctx.enter_context(tc.manual_schedule())
         const = ctx.enter_context(tc.tile_pool(name="const", bufs=1))
-        w1_pool = ctx.enter_context(tc.tile_pool(name="w1_pool", bufs=4))
-        byte_pool = ctx.enter_context(tc.tile_pool(name="byte_pool", bufs=3))
+        raw_pool = ctx.enter_context(tc.tile_pool(name="raw_pool", bufs=2))
+        byte_pool = ctx.enter_context(tc.tile_pool(name="byte_pool", bufs=5))
         work = ctx.enter_context(tc.tile_pool(name="work", bufs=3))
-        codes = ctx.enter_context(tc.tile_pool(name="codes", bufs=4))
-        w2_codes = ctx.enter_context(tc.tile_pool(name="w2_codes", bufs=10))
-        h_pool = ctx.enter_context(tc.tile_pool(name="h_pool", bufs=4))
-        hq_pool = ctx.enter_context(tc.tile_pool(name="hq_pool", bufs=8))
-        out_pool = ctx.enter_context(tc.tile_pool(name="out_pool", bufs=3))
-        ps_t = ctx.enter_context(tc.psum_pool(name="ps_t", bufs=2))
+        grp_pool = ctx.enter_context(tc.tile_pool(name="grp_pool", bufs=2))
+        w2_codes = ctx.enter_context(tc.tile_pool(name="w2_codes", bufs=16))
+        hq_pool = ctx.enter_context(tc.tile_pool(name="hq_pool", bufs=3))
+        out_pool = ctx.enter_context(tc.tile_pool(name="out_pool", bufs=2))
+        ps_t = ctx.enter_context(tc.psum_pool(name="ps_t", bufs=4))
         ps_h = ctx.enter_context(tc.psum_pool(name="ps_h", bufs=3))
-        ps_y = ctx.enter_context(tc.psum_pool(name="ps_y", bufs=2))
+        ps_y = ctx.enter_context(tc.psum_pool(name="ps_y", bufs=1))
 
-        w1_raw = {}
-        w2_raw = {}
+        w1_raw, w2_raw, b2_tile, turned = {}, {}, {}, {}
 
-        def load_w1(e, half):
-            raw = w1_pool.tile([P, 4, 1024], BF16, name="raw", align_bytes=64)
-            src = W1[e].rearrange("(p j) n -> p j n", j=4)
+        def load_direct(e, g):
+            if e == 0 and g == 0:
+                w1_raw["d"] = raw_pool.tile([P, 2 * G, 4, 512], BF16, name="raw", align_bytes=64)
+            nc.sync.dma_start(
+                out=w1_raw["d"][:, G * e + g, :, :],
+                in_=W1[e].rearrange("(p j) n -> p j n", j=4)[:, :, g * 512:(g + 1) * 512],
+            )
+
+        def load_pair(k):
+            raw = raw_pool.tile([P, P, P], BF16, name="raw", align_bytes=64)
+            for t in range(4):
+                for i in range(2):
+                    nc.sync.dma_start(
+                        out=raw[64 * i + t:64 * i + 64:4, :, :],
+                        in_=W1[2 * k + i].rearrange("(kk t) (b n) -> t b kk n", t=4, n=P)[t],
+                    )
+            w1_raw[k] = raw
+
+        def load_w2(e, half):
+            wb = byte_pool.tile([P, 2, 2048], U8, name="wb", align_bytes=64)
+            src = W2_bytes[e].rearrange("(g p s) n -> p g (s n)", p=P, s=4)[:, 2 * half:2 * half + 2, :]
             if e == 0 and half == 0:
-                for q in range(2):
-                    nc.sync.dma_start(out=raw[:, :, q * 512:(q + 1) * 512], in_=src[:, :, q * 512:(q + 1) * 512])
+                for g in range(2):
+                    nc.sync.dma_start(out=wb[:, g, :], in_=src[:, g, :])
             else:
-                nc.sync.dma_start(out=raw[:], in_=src[:, :, half * 1024:(half + 1) * 1024])
-            w1_raw[e, half] = raw
+                nc.sync.dma_start(out=wb[:], in_=src)
+            w2_raw[e, half] = wb
 
-        def load_w2(e):
-            wb = byte_pool.tile([P, G, 2048], U8, name="wb", align_bytes=64)
-            src = W2_bytes[e].rearrange("(g p s) n -> p g (s n)", p=P, s=4)
-            nc.sync.dma_start(out=wb[:], in_=src)
-            w2_raw[e] = wb
-
-        load_w1(0, 0)
-        b1_rows = const.tile([32, 512], BF16, name="b1_rows", align_bytes=64)
-        nc.sync.dma_start(out=b1_rows[:], in_=b1.rearrange("e (g c) -> (e g) c", c=512))
-        rows = const.tile([P, 512], F32, name="rows", align_bytes=64)
+        rows = out_pool.tile([P, 512], F32, name="rows", tag="y", align_bytes=64)
         nc.vector.memset(rows[:], 0.0)
         nc.sync.dma_start(out=rows[32:36, :], in_=W2_scale.rearrange("o (g c) z -> (o g) (c z)", c=512))
-        temp = const.tile([P, 1], BF16, name="temp", align_bytes=64)
-        nc.sync.dma_start(out=temp[:], in_=temperature.partition_broadcast(P))
+        b1_rows = out_pool.tile([32, 512], BF16, name="b1_rows", tag="b2_pair", align_bytes=64)
+        nc.sync.dma_start(out=b1_rows[:], in_=b1.rearrange("e (g c) -> (e g) c", c=512))
+        load_direct(0, 0)
+        load_w2(0, 0)
+        load_w2(0, 1)
         x_all = const.tile([P, E, D], BF16, name="x_all", align_bytes=64)
         x_src = x.rearrange("(e p) d -> p e d", p=P)
-        nc.sync.dma_start(out=x_all[:, 0:4, :], in_=x_src[:, 0:4, :])
-        load_w2(0)
-        load_w1(0, 1)
-        nc.sync.dma_start(out=x_all[:, 4:8, :], in_=x_src[:, 4:8, :])
+        nc.sync.dma_start(out=x_all[:, 0:2, :], in_=x_src[:, 0:2, :])
+        temp = const.tile([P, 1], BF16, name="temp", align_bytes=64)
+        nc.sync.dma_start(out=temp[:], in_=temperature.partition_broadcast(P))
+        for g in range(1, G):
+            load_direct(0, g)
+        load_w2(1, 0)
+        load_w2(1, 1)
+        for g in range(G):
+            load_direct(1, g)
 
         ident = const.tile([P, P], F32, name="ident", align_bytes=64)
         make_identity(nc, ident[:])
+        ident_b = const.tile([P, P], BF16, name="ident_b", align_bytes=64)
+        make_identity(nc, ident_b[:])
 
         nc.vector.tensor_copy(out=rows[0:32, :], in_=b1_rows[:])
-        rows_s = const.tile([P, 4, P], F32, name="rows_s", align_bytes=64)
+        rows_s = out_pool.tile([P, 4, P], F32, name="rows_s", tag="bg", align_bytes=64)
         nc.vector.tensor_copy(out=rows_s[:], in_=rows[:].rearrange("r (m s) -> r s m", s=4))
         col_ps = ps_t.tile([P, 4, P], F32, name="tp")
         for s in range(4):
@@ -101,71 +119,145 @@ def tile_moelayer_kernel(tc, x, W1, b1, W2_bytes, W2_scale, b2, temperature, out
         cols = const.tile([P, 36, 4], F32, name="cols", align_bytes=64)
         nc.vector.tensor_copy(out=cols[:], in_=col_ps[:, :, 0:36].rearrange("p s r -> p r s"))
 
-        clamped = const.tile([P, 1], F32, name="clamped", align_bytes=64)
-        nc.vector.tensor_scalar_min(clamped[:], temp[:], CLAMP_MAX)
-        gain = const.tile([P, 1], F32, name="gain", align_bytes=64)
-        nc.scalar.activation(out=gain[:], in_=clamped[:], func=ACT.Exp)
-
         xq = const.tile([P, E, TOK], U32, name="xq", align_bytes=64)
         xs = const.tile([P, E, TOK], U8, name="xs", align_bytes=64)
+        xg_t, gain = {}, const.tile([P, 1], F32, name="gain", align_bytes=64)
 
-        def x_pair(k):
+        def gain_calc():
+            clamped = const.tile([P, 1], F32, name="clamped", align_bytes=64)
+            nc.vector.tensor_scalar_min(clamped[:], temp[:], CLAMP_MAX)
+            nc.scalar.activation(out=gain[:], in_=clamped[:], func=ACT.Exp)
+
+        def x_turn(k):
             tp = ps_t.tile([P, 4, P], F32, name="tp")
             for i in range(2):
                 words = x_all[:, 2 * k + i, :].bitcast(F32)
                 for u in range(2):
                     nc.tensor.transpose(tp[:, 2 * i + u, :], words[:, u:256:2], ident[:])
-            xg = work.tile([P, 2, TOK, 4], BF16, name="xg", align_bytes=64)
+            xg = work.tile([P, 2, TOK, 4], BF16, name="xg", align_bytes=64, bufs=1)
             for i in range(2):
-                nc.vector.tensor_copy(
-                    out=xg[:, i, :, :].bitcast(F32),
-                    in_=tp[:, 2 * i:2 * i + 2, :].rearrange("p u r -> p r u"),
-                )
+                copy("s", xg[:, i, :, :].bitcast(F32), tp[:, 2 * i:2 * i + 2, :].rearrange("p u r -> p r u"))
+            xg_t[k] = xg
+
+        def x_quantise(k):
             nc.vector.quantize_mx(
                 out=xq[:, 2 * k:2 * k + 2, :].rearrange("p e r -> p (e r)").bitcast(FP8X4),
                 scales=xs[:, 2 * k:2 * k + 2, :].rearrange("p e r -> p (e r)"),
-                in_=xg[:].rearrange("p e r t -> p (e r t)"),
+                in_=xg_t[k][:].rearrange("p e r t -> p (e r t)"),
             )
-            use("v", 2 * 230 + 240)
 
-        b2_all = const.tile([P, E * D], BF16, name="b2_all", align_bytes=64)
+        w1_grp, w1_cod, w2_pl, w2_grp, w2_cod, h_ps, h_pl, h_grp, h_cod, y_ps, b2g = ({} for i in range(11))
 
-        w1_grp, w1_codes, w2_pl, w2_grp, w2_cod, h_ps, h_pl, h_grp, h_cod, y_ps, b2g = ({} for i in range(11))
-
-        def w1_interleave(e, g):
-            raw = w1_raw[e, g // 2]
-            grp = work.tile([P, 4, P, 4], BF16, name="w1g", align_bytes=64)
-            src = raw[:, :, (g % 2) * 512:(g % 2 + 1) * 512].rearrange("p j (m s) -> p m s j", s=4)
-            copy(pick(1080, 2050), grp[:].rearrange("p s m j -> p m s j"), src)
+        def direct_interleave(e, g):
+            grp = grp_pool.tile([P, 4, P, 4], BF16, name="w1g", align_bytes=64)
+            src = w1_raw["d"][:, G * e + g, :, :].rearrange("p j (m s) -> p m s j", s=4)
+            dst = grp[:].rearrange("p s m j -> p m s j")
+            nc.scalar.copy(out=dst[:, :, 0:2, :], in_=src[:, :, 0:2, :])
+            nc.vector.tensor_copy(out=dst[:, :, 2:4, :], in_=src[:, :, 2:4, :])
             w1_grp[e, g] = grp
 
-        def w1_quantise(e, g):
-            q = codes.tile([P, 512], U32, name="w1q", align_bytes=64)
-            sc = codes.tile([P, 512], U8, name="w1s", align_bytes=64)
+        def direct_quantise(e, g):
+            q = grp_pool.tile([P, 512], U32, name="w1q", align_bytes=64)
+            sc = grp_pool.tile([P, 512], U8, name="w1s", align_bytes=64)
             nc.vector.quantize_mx(
                 out=q[:].bitcast(FP8X4), scales=sc[:],
                 in_=w1_grp[e, g][:].rearrange("p s m j -> p (s m j)"),
             )
-            use("v", 480)
-            w1_codes[e, g] = (q, sc)
+            w1_cod[e, g] = (q, sc)
+
+        def direct_mm1(e, g):
+            q, sc = w1_cod[e, g]
+            ph = ps_h.tile([P, 4, TOK], F32, name="ph")
+            for s in range(4):
+                nc.tensor.matmul_mx(
+                    out=ph[:, s, :],
+                    lhsT=q[:, s * P:(s + 1) * P].bitcast(FP8X4), lhsT_scale=sc[:, s * P:(s + 1) * P],
+                    rhs=xq[:, e, :].bitcast(FP8X4), rhs_scale=xs[:, e, :],
+                    start=True, stop=True,
+                )
+            for s in range(4):
+                h_ps[e, g, s] = ph[:, s, :]
+
+        def turn(k, s, mb):
+            tp = ps_t.tile([P, 8, P], BF16, name="tp")
+            for i in range(8):
+                nc.tensor.transpose(tp[:, i, :], w1_raw[k][:, :, (mb * 8 + i) * 4 + s], ident_b[:])
+            turned[k, s, mb] = tp
+
+        def turned_copy(k, s, mb):
+            if mb == 0:
+                w1_grp[k, s, "t"] = grp_pool.tile([P, 32, 32, 4], BF16, name="w1g", align_bytes=64)
+            grp, tp = w1_grp[k, s, "t"], turned[k, s, mb]
+            copy(
+                "s",
+                grp[:, :, mb * 8:(mb + 1) * 8, :].rearrange("p a i t -> p a (i t)").bitcast(F32).rearrange("p a (i w) -> p a i w", w=2),
+                tp[:].rearrange("p i q -> p (i q)").bitcast(F32).rearrange("p (i a w) -> p a i w", i=8, w=2),
+            )
+
+        def turned_quantise(k, s):
+            q = grp_pool.tile([P, 1024], U32, name="w1q", align_bytes=64)
+            sc = grp_pool.tile([P, 1024], U8, name="w1s", align_bytes=64)
+            nc.vector.quantize_mx(
+                out=q[:].bitcast(FP8X4), scales=sc[:],
+                in_=w1_grp[k, s, "t"][:].rearrange("p a m t -> p (a m t)"),
+            )
+            w1_cod[k, s, "t"] = (q, sc)
+
+        def turned_mm1(k, s):
+            q, sc = w1_cod[k, s, "t"]
+            for i in range(2):
+                ph = ps_h.tile([P, 4, TOK], F32, name="ph")
+                for g in range(G):
+                    c = (4 * i + g) * P
+                    nc.tensor.matmul_mx(
+                        out=ph[:, g, :],
+                        lhsT=q[:, c:c + P].bitcast(FP8X4), lhsT_scale=sc[:, c:c + P],
+                        rhs=xq[:, 2 * k + i, :].bitcast(FP8X4), rhs_scale=xs[:, 2 * k + i, :],
+                        start=True, stop=True,
+                    )
+                for g in range(G):
+                    h_ps[2 * k + i, g, s] = ph[:, g, :]
+
+        def h_relu(e, g, s):
+            if e not in h_pl:
+                h_pl[e] = work.tile([P, 4, G * TOK], BF16, name="hp", align_bytes=64, bufs=4)
+            nc.scalar.activation(
+                out=h_pl[e][:, s, g * TOK:(g + 1) * TOK], in_=h_ps[e, g, s],
+                func=ACT.Relu, bias=cols[:, 4 * e + g, s:s + 1],
+            )
+
+        def h_interleave(e):
+            grp = work.tile([P, G * TOK, 4], BF16, name="hg", align_bytes=64, bufs=2)
+            split_copy(
+                grp[:].rearrange("p (c i) s -> p c s i", i=4),
+                h_pl[e][:].rearrange("p s (c i) -> p c s i", i=4),
+                64 if e >= 6 else H_SPLIT,
+            )
+            h_grp[e] = grp
+
+        def h_quantise(e):
+            q = hq_pool.tile([P, G * TOK], U32, name="hq", align_bytes=64)
+            sc = hq_pool.tile([P, G * TOK], U8, name="hs", align_bytes=64)
+            nc.vector.quantize_mx(
+                out=q[:].bitcast(FP8X4), scales=sc[:], in_=h_grp[e][:].rearrange("p n s -> p (n s)")
+            )
+            h_cod[e] = (q, sc)
 
         def w2_widen(e, g):
-            plane = work.tile([P, 4, 512], BF16, name="w2p", align_bytes=64)
+            plane = work.tile([P, 4, 512], BF16, name="w2p", align_bytes=64, bufs=3)
             for s in range(4):
-                src = w2_raw[e][:, g, s * 512:(s + 1) * 512].bitcast(FP8)
-                col = cols[:, 32 + g, s:s + 1]
-                if pick(230, 450) == "v":
-                    nc.vector.tensor_scalar(out=plane[:, s, :], in0=src, scalar1=col, scalar2=None, op0=ALU.mult)
-                else:
-                    nc.scalar.activation(out=plane[:, s, :], in_=src, func=ACT.Copy, scale=col)
+                nc.vector.tensor_scalar(
+                    out=plane[:, s, :], in0=w2_raw[e, g // 2][:, g % 2, s * 512:(s + 1) * 512].bitcast(FP8),
+                    scalar1=cols[:, 32 + g, s:s + 1], scalar2=None, op0=ALU.mult,
+                )
             w2_pl[e, g] = plane
 
         def w2_interleave(e, g):
-            grp = work.tile([P, 512, 4], BF16, name="w2g", align_bytes=64)
-            copy(
-                pick(1080, 2050),
+            grp = work.tile([P, 512, 4], BF16, name="w2g", align_bytes=64, bufs=3)
+            split_copy(
                 grp[:].rearrange("p (c i) s -> p c s i", i=4),
                 w2_pl[e, g][:].rearrange("p s (c i) -> p c s i", i=4),
+                D_SPLIT if 4 * e + g < 8 else W_SPLIT,
             )
             w2_grp[e, g] = grp
 
@@ -175,68 +267,33 @@ def tile_moelayer_kernel(tc, x, W1, b1, W2_bytes, W2_scale, b2, temperature, out
             nc.vector.quantize_mx(
                 out=q[:].bitcast(FP8X4), scales=sc[:], in_=w2_grp[e, g][:].rearrange("p n s -> p (n s)")
             )
-            use("v", 480)
             w2_cod[e, g] = (q, sc)
-
-        def mm1(e, g):
-            q, sc = w1_codes[e, g]
-            ph = ps_h.tile([P, 4, TOK], F32, name="ph")
-            for s in range(4):
-                nc.tensor.matmul_mx(
-                    out=ph[:, s, :],
-                    lhsT=q[:, s * P:(s + 1) * P].bitcast(FP8X4), lhsT_scale=sc[:, s * P:(s + 1) * P],
-                    rhs=xq[:, e, :].bitcast(FP8X4), rhs_scale=xs[:, e, :],
-                    start=True, stop=True,
-                )
-            h_ps[e, g] = ph
-
-        def h_relu(e, g):
-            ph = h_ps[e, g]
-            plane = h_pool.tile([P, 4, TOK], BF16, name="hp", align_bytes=64)
-            for s in range(4):
-                nc.scalar.activation(
-                    out=plane[:, s, :], in_=ph[:, s, :], func=ACT.Relu, bias=cols[:, 4 * e + g, s:s + 1]
-                )
-            use("s", 600)
-            h_pl[e, g] = plane
-
-        def h_interleave(e, g):
-            grp = h_pool.tile([P, TOK, 4], BF16, name="hg", align_bytes=64)
-            copy(
-                pick(285, 530),
-                grp[:].rearrange("p (c i) s -> p c s i", i=4),
-                h_pl[e, g][:].rearrange("p s (c i) -> p c s i", i=4),
-            )
-            h_grp[e, g] = grp
-
-        def h_quantise(e, g):
-            q = hq_pool.tile([P, TOK], U32, name="hq", align_bytes=64)
-            sc = hq_pool.tile([P, TOK], U8, name="hs", align_bytes=64)
-            nc.vector.quantize_mx(
-                out=q[:].bitcast(FP8X4), scales=sc[:], in_=h_grp[e, g][:].rearrange("p n s -> p (n s)")
-            )
-            use("v", 140)
-            h_cod[e, g] = (q, sc)
 
         def mm2(e):
             py = ps_y.tile([TOK, D], F32, name="py")
+            hq, hs = h_cod[e]
             for g in range(G):
-                hq, hs = h_cod[e, g]
                 wq, ws = w2_cod[e, g]
+                c = slice(g * TOK, (g + 1) * TOK)
                 nc.tensor.matmul_mx(
-                    out=py[:], lhsT=hq[:].bitcast(FP8X4), lhsT_scale=hs[:],
+                    out=py[:], lhsT=hq[:, c].bitcast(FP8X4), lhsT_scale=hs[:, c],
                     rhs=wq[:].bitcast(FP8X4), rhs_scale=ws[:],
                     start=(g == 0), stop=(g == G - 1),
                 )
             y_ps[e] = py
 
+        def b2_load(k):
+            b2_tile[k] = out_pool.tile([P, 2 * D], BF16, name="b2_pair", align_bytes=64)
+            nc.sync.dma_start(
+                out=b2_tile[k][:],
+                in_=b2[2 * k:2 * k + 2, :].rearrange("e d -> (e d)").partition_broadcast(P),
+            )
+
         def bias2(e):
             bg = out_pool.tile([P, D], F32, name="bg", align_bytes=64)
-            src = b2_all[:, e * D:(e + 1) * D]
-            if pick(240, 450) == "v":
-                nc.vector.tensor_scalar(out=bg[:], in0=src, scalar1=gain[:], scalar2=None, op0=ALU.mult)
-            else:
-                nc.scalar.activation(out=bg[:], in_=src, func=ACT.Copy, scale=gain[:])
+            nc.vector.tensor_scalar(
+                out=bg[:], in0=b2_tile[e // 2][:, (e % 2) * D:(e % 2 + 1) * D], scalar1=gain[:], scalar2=None, op0=ALU.mult
+            )
             b2g[e] = bg
 
         def store(e):
@@ -244,50 +301,129 @@ def tile_moelayer_kernel(tc, x, W1, b1, W2_bytes, W2_scale, b2, temperature, out
             nc.vector.scalar_tensor_tensor(
                 out=y[:], in0=y_ps[e][:], scalar=gain[:], in1=b2g[e][:], op0=ALU.mult, op1=ALU.add
             )
-            use("v", 450)
             nc.sync.dma_start(out=out[e * TOK:(e + 1) * TOK, :], in_=y[:])
 
+        h_jobs = {}
+
+        def finish(n, experts):
+            for j, e in enumerate(experts):
+                h_jobs.setdefault(n + 1 + j, []).append(lambda e=e: h_interleave(e))
+                h_jobs.setdefault(n + 2 + j, []).append(lambda e=e: h_output(e))
+                h_jobs.setdefault(n + 3 + j, []).append(lambda e=e: store(e))
+
+        def h_output(e):
+            h_quantise(e)
+            bias2(e)
+            mm2(e)
+
+        def h_beat(n):
+            for job in h_jobs.pop(n, []):
+                job()
+
         units = [(e, g) for e in range(E) for g in range(G)]
-        n_units = len(units)
+        nc.sync.dma_start(out=x_all[:, 2:8, :], in_=x_src[:, 2:8, :])
+        b2_load(0)
 
-        def at(i):
-            return units[i] if 0 <= i < n_units else None
+        for n in range(8):
+            u = units[n]
+            if n == 2:
+                load_w2(2, 0)
+                load_w2(2, 1)
+                load_pair(1)
+            if n == 1:
+                x_quantise(0)
+            w2_widen(*u)
+            if n >= 1:
+                w2_quantise(*units[n - 1])
+                direct_quantise(*units[n - 1])
+                direct_mm1(*units[n - 1])
+            h_beat(n)
+            direct_interleave(*u)
+            if n == 0:
+                x_turn(0)
+            if n >= 2:
+                for s in range(4):
+                    h_relu(*units[n - 2], s)
+                if units[n - 2][1] == G - 1:
+                    finish(n, [units[n - 2][0]])
+            w2_interleave(*u)
+            if 5 <= n < 8:
+                x_quantise(n - 4)
+            if 4 <= n < 7:
+                x_turn(n - 3)
+            if n == 3:
+                gain_calc()
+        load_w2(3, 0)
+        load_w2(3, 1)
+        direct_quantise(*units[7])
+        direct_mm1(*units[7])
+        for s in range(4):
+            h_relu(*units[6], s)
+        fill = units[8:8 + FILL]
+        w2_widen(*fill[0])
+        w2_widen(*fill[1])
+        w2_quantise(*units[7])
+        w2_interleave(*fill[0])
+        for s in range(4):
+            h_relu(*units[7], s)
+        finish(8, [1])
+        w2_interleave(*fill[1])
+        h_beat(8)
+        for mb in range(4):
+            turn(1, 0, mb)
+        for j in range(2, FILL):
+            w2_widen(*fill[j])
+            w2_quantise(*fill[j - 2])
+            w2_interleave(*fill[j])
 
-        for i in range(n_units + 8):
-            u = at(i)
-            if u is not None:
-                e, g = u
-                if g == 0 and e + 1 < E:
-                    load_w1(e + 1, 0)
-                    load_w2(e + 1)
-                    load_w1(e + 1, 1)
-                if e == 0 and g == 2:
-                    nc.sync.dma_start(out=b2_all[:], in_=b2.rearrange("e d -> (e d)").partition_broadcast(P))
-                w1_interleave(e, g)
-                if i < 4:
-                    x_pair(i)
-                w2_widen(e, g)
-            u = at(i - 1)
-            if u is not None:
-                w1_quantise(*u)
-                w2_interleave(*u)
-            u = at(i - 2)
-            if u is not None:
+        load_w2(4, 0)
+        load_w2(4, 1)
+        load_pair(2)
+        ticks = [(k, s) for k in range(1, 4) for s in range(4)]
+        done = 8 + FILL
+        before = fill[FILL - 2:]
+        for i, (k, s) in enumerate(ticks):
+            n = 9 + i
+            now = units[done:done + PER_TICK[i]]
+            done += len(now)
+            for mb in range(4):
+                turned_copy(k, s, mb)
+                if i + 1 < len(ticks):
+                    turn(*ticks[i + 1], mb)
+            if now:
+                w2_widen(*now[0])
+            for u in before:
                 w2_quantise(*u)
-                mm1(*u)
-            u = at(i - 3)
-            if u is not None:
-                h_relu(*u)
-            u = at(i - 4)
-            if u is not None:
-                h_interleave(*u)
-            u = at(i - 5)
-            if u is not None:
-                h_quantise(*u)
-                if u[1] == 2:
-                    bias2(u[0])
-                if u[1] == G - 1:
-                    mm2(u[0])
-            u = at(i - 6)
-            if u is not None and u[1] == G - 1:
-                store(u[0])
+            if len(now) > 1:
+                w2_widen(*now[1])
+            turned_quantise(k, s)
+            if i >= 1:
+                k0, s0 = ticks[i - 1]
+                for r in range(8):
+                    h_relu(2 * k0 + r // 4, r % 4, s0)
+                if s0 == 3:
+                    finish(n, [2 * k0, 2 * k0 + 1])
+            turned_mm1(k, s)
+            for u in now:
+                w2_interleave(*u)
+            h_beat(n)
+            before = now
+            if i in (1, 3, 5):
+                load_w2(5 + (i - 1) // 2, 0)
+                load_w2(5 + (i - 1) // 2, 1)
+            if i == 4:
+                load_pair(3)
+            if i in (0, 4, 8):
+                b2_load(1 + i // 4)
+        for u in before:
+            w2_quantise(*u)
+        k0, s0 = ticks[-1]
+        for r in range(8):
+            h_relu(2 * k0 + r // 4, r % 4, s0)
+        for e in (2 * k0, 2 * k0 + 1):
+            h_interleave(e)
+        h_beat(9 + len(ticks))
+        h_beat(10 + len(ticks))
+        for e in (2 * k0, 2 * k0 + 1):
+            h_output(e)
+            store(e)

@@ -17,10 +17,11 @@ N, D, H, E = 1024, 512, 2048, 8
 P = 128
 TOK = N // E
 G = H // 512
-FILL = 4
-PER_TICK = (2, 2, 2, 2, 2, 2, 2, 2, 1, 1, 1, 1)
-D_SPLIT = 84
-W_SPLIT = 82
+DRING = 8
+Q_LAG = 2
+W_LAG = 2
+RELU_LAG = 3
+D_ENG = "sssv"
 H_SPLIT = 0
 CLAMP_MAX = float(math.log(100.0))
 FLOPS = 2 * N * D * H * 2
@@ -45,35 +46,24 @@ def tile_moelayer_kernel(tc, x, W1, b1, W2_bytes, W2_scale, b2, temperature, out
         ctx.enter_context(tc.manual_schedule())
         const = ctx.enter_context(tc.tile_pool(name="const", bufs=1))
         raw_pool = ctx.enter_context(tc.tile_pool(name="raw_pool", bufs=2))
-        byte_pool = ctx.enter_context(tc.tile_pool(name="byte_pool", bufs=5))
+        byte_pool = ctx.enter_context(tc.tile_pool(name="byte_pool", bufs=6))
         work = ctx.enter_context(tc.tile_pool(name="work", bufs=3))
-        grp_pool = ctx.enter_context(tc.tile_pool(name="grp_pool", bufs=2))
-        w2_codes = ctx.enter_context(tc.tile_pool(name="w2_codes", bufs=16))
+        grp_pool = ctx.enter_context(tc.tile_pool(name="grp_pool", bufs=4))
+        w2_codes = ctx.enter_context(tc.tile_pool(name="w2_codes", bufs=10))
         hq_pool = ctx.enter_context(tc.tile_pool(name="hq_pool", bufs=3))
         out_pool = ctx.enter_context(tc.tile_pool(name="out_pool", bufs=2))
-        ps_t = ctx.enter_context(tc.psum_pool(name="ps_t", bufs=4))
-        ps_h = ctx.enter_context(tc.psum_pool(name="ps_h", bufs=3))
-        ps_y = ctx.enter_context(tc.psum_pool(name="ps_y", bufs=1))
+        ps_t = ctx.enter_context(tc.psum_pool(name="ps_t", bufs=2))
+        ps_h = ctx.enter_context(tc.psum_pool(name="ps_h", bufs=4))
+        ps_y = ctx.enter_context(tc.psum_pool(name="ps_y", bufs=2))
 
         w1_raw, w2_raw, b2_tile, turned = {}, {}, {}, {}
 
         def load_direct(e, g):
-            if e == 0 and g == 0:
-                w1_raw["d"] = raw_pool.tile([P, 2 * G, 4, 512], BF16, name="raw", align_bytes=64)
+            raw = raw_pool.tile([P, 4, 512], BF16, name="raw_d", align_bytes=64, bufs=DRING)
             nc.sync.dma_start(
-                out=w1_raw["d"][:, G * e + g, :, :],
-                in_=W1[e].rearrange("(p j) n -> p j n", j=4)[:, :, g * 512:(g + 1) * 512],
+                out=raw[:], in_=W1[e].rearrange("(p j) n -> p j n", j=4)[:, :, g * 512:(g + 1) * 512]
             )
-
-        def load_pair(k):
-            raw = raw_pool.tile([P, P, P], BF16, name="raw", align_bytes=64)
-            for t in range(4):
-                for i in range(2):
-                    nc.sync.dma_start(
-                        out=raw[64 * i + t:64 * i + 64:4, :, :],
-                        in_=W1[2 * k + i].rearrange("(kk t) (b n) -> t b kk n", t=4, n=P)[t],
-                    )
-            w1_raw[k] = raw
+            w1_raw[e, g] = raw
 
         def load_w2(e, half):
             wb = byte_pool.tile([P, 2, 2048], U8, name="wb", align_bytes=64)
@@ -88,7 +78,7 @@ def tile_moelayer_kernel(tc, x, W1, b1, W2_bytes, W2_scale, b2, temperature, out
         rows = out_pool.tile([P, 512], F32, name="rows", tag="y", align_bytes=64)
         nc.vector.memset(rows[:], 0.0)
         nc.sync.dma_start(out=rows[32:36, :], in_=W2_scale.rearrange("o (g c) z -> (o g) (c z)", c=512))
-        b1_rows = out_pool.tile([32, 512], BF16, name="b1_rows", tag="b2_pair", align_bytes=64)
+        b1_rows = out_pool.tile([32, 512], BF16, name="b1_rows", tag="b2_row", align_bytes=64, bufs=4)
         nc.sync.dma_start(out=b1_rows[:], in_=b1.rearrange("e (g c) -> (e g) c", c=512))
         load_direct(0, 0)
         load_w2(0, 0)
@@ -101,14 +91,10 @@ def tile_moelayer_kernel(tc, x, W1, b1, W2_bytes, W2_scale, b2, temperature, out
         for g in range(1, G):
             load_direct(0, g)
         load_w2(1, 0)
-        load_w2(1, 1)
-        for g in range(G):
-            load_direct(1, g)
+        load_direct(1, 0)
 
         ident = const.tile([P, P], F32, name="ident", align_bytes=64)
         make_identity(nc, ident[:])
-        ident_b = const.tile([P, P], BF16, name="ident_b", align_bytes=64)
-        make_identity(nc, ident_b[:])
 
         nc.vector.tensor_copy(out=rows[0:32, :], in_=b1_rows[:])
         rows_s = out_pool.tile([P, 4, P], F32, name="rows_s", tag="bg", align_bytes=64)
@@ -150,10 +136,12 @@ def tile_moelayer_kernel(tc, x, W1, b1, W2_bytes, W2_scale, b2, temperature, out
 
         def direct_interleave(e, g):
             grp = grp_pool.tile([P, 4, P, 4], BF16, name="w1g", align_bytes=64)
-            src = w1_raw["d"][:, G * e + g, :, :].rearrange("p j (m s) -> p m s j", s=4)
+            src = w1_raw[e, g][:].rearrange("p j (m s) -> p m s j", s=4)
             dst = grp[:].rearrange("p s m j -> p m s j")
-            nc.scalar.copy(out=dst[:, :, 0:2, :], in_=src[:, :, 0:2, :])
-            nc.vector.tensor_copy(out=dst[:, :, 2:4, :], in_=src[:, :, 2:4, :])
+            if D_ENG[(G * e + g) % len(D_ENG)] == "v":
+                nc.vector.tensor_copy(out=dst, in_=src)
+            else:
+                nc.scalar.copy(out=dst, in_=src)
             w1_grp[e, g] = grp
 
         def direct_quantise(e, g):
@@ -177,46 +165,6 @@ def tile_moelayer_kernel(tc, x, W1, b1, W2_bytes, W2_scale, b2, temperature, out
                 )
             for s in range(4):
                 h_ps[e, g, s] = ph[:, s, :]
-
-        def turn(k, s, mb):
-            tp = ps_t.tile([P, 8, P], BF16, name="tp")
-            for i in range(8):
-                nc.tensor.transpose(tp[:, i, :], w1_raw[k][:, :, (mb * 8 + i) * 4 + s], ident_b[:])
-            turned[k, s, mb] = tp
-
-        def turned_copy(k, s, mb):
-            if mb == 0:
-                w1_grp[k, s, "t"] = grp_pool.tile([P, 32, 32, 4], BF16, name="w1g", align_bytes=64)
-            grp, tp = w1_grp[k, s, "t"], turned[k, s, mb]
-            copy(
-                "s",
-                grp[:, :, mb * 8:(mb + 1) * 8, :].rearrange("p a i t -> p a (i t)").bitcast(F32).rearrange("p a (i w) -> p a i w", w=2),
-                tp[:].rearrange("p i q -> p (i q)").bitcast(F32).rearrange("p (i a w) -> p a i w", i=8, w=2),
-            )
-
-        def turned_quantise(k, s):
-            q = grp_pool.tile([P, 1024], U32, name="w1q", align_bytes=64)
-            sc = grp_pool.tile([P, 1024], U8, name="w1s", align_bytes=64)
-            nc.vector.quantize_mx(
-                out=q[:].bitcast(FP8X4), scales=sc[:],
-                in_=w1_grp[k, s, "t"][:].rearrange("p a m t -> p (a m t)"),
-            )
-            w1_cod[k, s, "t"] = (q, sc)
-
-        def turned_mm1(k, s):
-            q, sc = w1_cod[k, s, "t"]
-            for i in range(2):
-                ph = ps_h.tile([P, 4, TOK], F32, name="ph")
-                for g in range(G):
-                    c = (4 * i + g) * P
-                    nc.tensor.matmul_mx(
-                        out=ph[:, g, :],
-                        lhsT=q[:, c:c + P].bitcast(FP8X4), lhsT_scale=sc[:, c:c + P],
-                        rhs=xq[:, 2 * k + i, :].bitcast(FP8X4), rhs_scale=xs[:, 2 * k + i, :],
-                        start=True, stop=True,
-                    )
-                for g in range(G):
-                    h_ps[2 * k + i, g, s] = ph[:, g, :]
 
         def h_relu(e, g, s):
             if e not in h_pl:
@@ -244,20 +192,20 @@ def tile_moelayer_kernel(tc, x, W1, b1, W2_bytes, W2_scale, b2, temperature, out
             h_cod[e] = (q, sc)
 
         def w2_widen(e, g):
-            plane = work.tile([P, 4, 512], BF16, name="w2p", align_bytes=64, bufs=3)
-            for s in range(4):
+            plane = work.tile([P, 2, 512, 2], BF16, name="w2p", align_bytes=64, bufs=3)
+            for s in (0, 2, 1, 3):
                 nc.vector.tensor_scalar(
-                    out=plane[:, s, :], in0=w2_raw[e, g // 2][:, g % 2, s * 512:(s + 1) * 512].bitcast(FP8),
+                    out=plane[:, s // 2, :, s % 2],
+                    in0=w2_raw[e, g // 2][:, g % 2, s * 512:(s + 1) * 512].bitcast(FP8),
                     scalar1=cols[:, 32 + g, s:s + 1], scalar2=None, op0=ALU.mult,
                 )
             w2_pl[e, g] = plane
 
         def w2_interleave(e, g):
-            grp = work.tile([P, 512, 4], BF16, name="w2g", align_bytes=64, bufs=3)
-            split_copy(
-                grp[:].rearrange("p (c i) s -> p c s i", i=4),
-                w2_pl[e, g][:].rearrange("p s (c i) -> p c s i", i=4),
-                D_SPLIT if 4 * e + g < 8 else W_SPLIT,
+            grp = work.tile([P, 512, 4], BF16, name="w2g", align_bytes=64, bufs=4)
+            nc.scalar.copy(
+                out=grp[:].bitcast(F32),
+                in_=w2_pl[e, g][:].rearrange("p h n l -> p h (n l)").bitcast(F32).rearrange("p h n -> p n h"),
             )
             w2_grp[e, g] = grp
 
@@ -282,17 +230,15 @@ def tile_moelayer_kernel(tc, x, W1, b1, W2_bytes, W2_scale, b2, temperature, out
                 )
             y_ps[e] = py
 
-        def b2_load(k):
-            b2_tile[k] = out_pool.tile([P, 2 * D], BF16, name="b2_pair", align_bytes=64)
-            nc.sync.dma_start(
-                out=b2_tile[k][:],
-                in_=b2[2 * k:2 * k + 2, :].rearrange("e d -> (e d)").partition_broadcast(P),
-            )
+        def b2_load(experts):
+            for e in experts:
+                b2_tile[e] = out_pool.tile([P, D], BF16, name="b2_row", align_bytes=64, bufs=4)
+                nc.sync.dma_start(out=b2_tile[e][:], in_=b2[e, :].partition_broadcast(P))
 
         def bias2(e):
             bg = out_pool.tile([P, D], F32, name="bg", align_bytes=64)
             nc.vector.tensor_scalar(
-                out=bg[:], in0=b2_tile[e // 2][:, (e % 2) * D:(e % 2 + 1) * D], scalar1=gain[:], scalar2=None, op0=ALU.mult
+                out=bg[:], in0=b2_tile[e][:], scalar1=gain[:], scalar2=None, op0=ALU.mult
             )
             b2g[e] = bg
 
@@ -309,7 +255,7 @@ def tile_moelayer_kernel(tc, x, W1, b1, W2_bytes, W2_scale, b2, temperature, out
             for j, e in enumerate(experts):
                 h_jobs.setdefault(n + 1 + j, []).append(lambda e=e: h_interleave(e))
                 h_jobs.setdefault(n + 2 + j, []).append(lambda e=e: h_output(e))
-                h_jobs.setdefault(n + 3 + j, []).append(lambda e=e: store(e))
+                h_jobs.setdefault(n + 3 + j, []).insert(0, lambda e=e: store(e))
 
         def h_output(e):
             h_quantise(e)
@@ -321,109 +267,48 @@ def tile_moelayer_kernel(tc, x, W1, b1, W2_bytes, W2_scale, b2, temperature, out
                 job()
 
         units = [(e, g) for e in range(E) for g in range(G)]
-        nc.sync.dma_start(out=x_all[:, 2:8, :], in_=x_src[:, 2:8, :])
-        b2_load(0)
+        n_units = len(units)
 
-        for n in range(8):
-            u = units[n]
-            if n == 2:
-                load_w2(2, 0)
-                load_w2(2, 1)
-                load_pair(1)
+        def late(n, lag):
+            return units[n - lag] if 0 <= n - lag < n_units else None
+
+        for n in range(n_units + RELU_LAG + 4):
+            u = late(n, 0)
+            if u:
+                w2_widen(*u)
             if n == 1:
                 x_quantise(0)
-            w2_widen(*u)
-            if n >= 1:
-                w2_quantise(*units[n - 1])
-                direct_quantise(*units[n - 1])
-                direct_mm1(*units[n - 1])
-            h_beat(n)
-            direct_interleave(*u)
-            if n == 0:
-                x_turn(0)
-            if n >= 2:
+            v = late(n, Q_LAG)
+            if v:
+                direct_quantise(*v)
+                direct_mm1(*v)
+            v = late(n, W_LAG)
+            if v:
+                w2_quantise(*v)
+            v = late(n, RELU_LAG)
+            if v:
                 for s in range(4):
-                    h_relu(*units[n - 2], s)
-                if units[n - 2][1] == G - 1:
-                    finish(n, [units[n - 2][0]])
-            w2_interleave(*u)
-            if 5 <= n < 8:
-                x_quantise(n - 4)
-            if 4 <= n < 7:
-                x_turn(n - 3)
-            if n == 3:
-                gain_calc()
-        load_w2(3, 0)
-        load_w2(3, 1)
-        direct_quantise(*units[7])
-        direct_mm1(*units[7])
-        for s in range(4):
-            h_relu(*units[6], s)
-        fill = units[8:8 + FILL]
-        w2_widen(*fill[0])
-        w2_widen(*fill[1])
-        w2_quantise(*units[7])
-        w2_interleave(*fill[0])
-        for s in range(4):
-            h_relu(*units[7], s)
-        finish(8, [1])
-        w2_interleave(*fill[1])
-        h_beat(8)
-        for mb in range(4):
-            turn(1, 0, mb)
-        for j in range(2, FILL):
-            w2_widen(*fill[j])
-            w2_quantise(*fill[j - 2])
-            w2_interleave(*fill[j])
-
-        load_w2(4, 0)
-        load_w2(4, 1)
-        load_pair(2)
-        ticks = [(k, s) for k in range(1, 4) for s in range(4)]
-        done = 8 + FILL
-        before = fill[FILL - 2:]
-        for i, (k, s) in enumerate(ticks):
-            n = 9 + i
-            now = units[done:done + PER_TICK[i]]
-            done += len(now)
-            for mb in range(4):
-                turned_copy(k, s, mb)
-                if i + 1 < len(ticks):
-                    turn(*ticks[i + 1], mb)
-            if now:
-                w2_widen(*now[0])
-            for u in before:
-                w2_quantise(*u)
-            if len(now) > 1:
-                w2_widen(*now[1])
-            turned_quantise(k, s)
-            if i >= 1:
-                k0, s0 = ticks[i - 1]
-                for r in range(8):
-                    h_relu(2 * k0 + r // 4, r % 4, s0)
-                if s0 == 3:
-                    finish(n, [2 * k0, 2 * k0 + 1])
-            turned_mm1(k, s)
-            for u in now:
-                w2_interleave(*u)
+                    h_relu(*v, s)
+                if v[1] == G - 1:
+                    finish(n, [v[0]])
             h_beat(n)
-            before = now
-            if i in (1, 3, 5):
-                load_w2(5 + (i - 1) // 2, 0)
-                load_w2(5 + (i - 1) // 2, 1)
-            if i == 4:
-                load_pair(3)
-            if i in (0, 4, 8):
-                b2_load(1 + i // 4)
-        for u in before:
-            w2_quantise(*u)
-        k0, s0 = ticks[-1]
-        for r in range(8):
-            h_relu(2 * k0 + r // 4, r % 4, s0)
-        for e in (2 * k0, 2 * k0 + 1):
-            h_interleave(e)
-        h_beat(9 + len(ticks))
-        h_beat(10 + len(ticks))
-        for e in (2 * k0, 2 * k0 + 1):
-            h_output(e)
-            store(e)
+            if u:
+                direct_interleave(*u)
+                if n == 0:
+                    x_turn(0)
+                w2_interleave(*u)
+                e, g = u
+                if e in (1, 2, 3) and g == 0:
+                    x_turn(e)
+                if e in (1, 2, 3) and g == 1:
+                    x_quantise(e)
+                if n == 3:
+                    gain_calc()
+                if n + 5 < n_units:
+                    load_direct(*units[n + 5])
+                if g % 2 == 1 and n + 5 < n_units:
+                    load_w2(units[n + 5][0], units[n + 5][1] // 2)
+                if g == 0:
+                    b2_load((e,))
+                if n == 1:
+                    nc.sync.dma_start(out=x_all[:, 2:8, :], in_=x_src[:, 2:8, :])

import math
from contextlib import ExitStack

import concourse.mybir as mybir
from concourse.masks import make_identity

F32 = mybir.dt.float32
BF16 = mybir.dt.bfloat16
U32 = mybir.dt.uint32
U8 = mybir.dt.uint8
FP8 = mybir.dt.float8_e4m3fn
FP8X4 = mybir.dt.float8_e4m3fn_x4
ALU = mybir.AluOpType
ACT = mybir.ActivationFunctionType

N, D, H, E = 1024, 512, 2048, 8
P = 128
TOK = N // E
G = H // 512
DRING = 8
Q_LAG = 2
W_LAG = 2
RELU_LAG = 3
D_ENG = "sssv"
H_SPLIT = 0
CLAMP_MAX = float(math.log(100.0))
FLOPS = 2 * N * D * H * 2


def tile_moelayer_kernel(tc, x, W1, b1, W2_bytes, W2_scale, b2, temperature, out):
    nc = tc.nc

    def split_copy(dst, src, s_part):
        if s_part > 0:
            nc.scalar.copy(out=dst[:, 0:s_part], in_=src[:, 0:s_part])
        if s_part < dst.shape[1]:
            nc.vector.tensor_copy(out=dst[:, s_part:dst.shape[1]], in_=src[:, s_part:dst.shape[1]])

    def copy(engine, dst, src):
        if engine == "v":
            nc.vector.tensor_copy(out=dst, in_=src)
        else:
            nc.scalar.copy(out=dst, in_=src)

    with ExitStack() as ctx:
        ctx.enter_context(tc.manual_schedule())
        const = ctx.enter_context(tc.tile_pool(name="const", bufs=1))
        raw_pool = ctx.enter_context(tc.tile_pool(name="raw_pool", bufs=2))
        byte_pool = ctx.enter_context(tc.tile_pool(name="byte_pool", bufs=6))
        work = ctx.enter_context(tc.tile_pool(name="work", bufs=3))
        grp_pool = ctx.enter_context(tc.tile_pool(name="grp_pool", bufs=4))
        w2_codes = ctx.enter_context(tc.tile_pool(name="w2_codes", bufs=10))
        hq_pool = ctx.enter_context(tc.tile_pool(name="hq_pool", bufs=3))
        out_pool = ctx.enter_context(tc.tile_pool(name="out_pool", bufs=2))
        ps_t = ctx.enter_context(tc.psum_pool(name="ps_t", bufs=2))
        ps_h = ctx.enter_context(tc.psum_pool(name="ps_h", bufs=4))
        ps_y = ctx.enter_context(tc.psum_pool(name="ps_y", bufs=2))

        w1_raw, w2_raw, b2_tile, turned = {}, {}, {}, {}

        def load_direct(e, g):
            raw = raw_pool.tile([P, 4, 512], BF16, name="raw_d", align_bytes=64, bufs=DRING)
            nc.sync.dma_start(
                out=raw[:], in_=W1[e].rearrange("(p j) n -> p j n", j=4)[:, :, g * 512:(g + 1) * 512]
            )
            w1_raw[e, g] = raw

        def load_w2(e, half):
            wb = byte_pool.tile([P, 2, 2048], U8, name="wb", align_bytes=64)
            src = W2_bytes[e].rearrange("(g p s) n -> p g (s n)", p=P, s=4)[:, 2 * half:2 * half + 2, :]
            if e == 0 and half == 0:
                for g in range(2):
                    nc.sync.dma_start(out=wb[:, g, :], in_=src[:, g, :])
            else:
                nc.sync.dma_start(out=wb[:], in_=src)
            w2_raw[e, half] = wb

        rows = out_pool.tile([P, 512], F32, name="rows", tag="y", align_bytes=64)
        nc.vector.memset(rows[:], 0.0)
        nc.sync.dma_start(out=rows[32:36, :], in_=W2_scale.rearrange("o (g c) z -> (o g) (c z)", c=512))
        b1_rows = out_pool.tile([32, 512], BF16, name="b1_rows", tag="b2_row", align_bytes=64, bufs=4)
        nc.sync.dma_start(out=b1_rows[:], in_=b1.rearrange("e (g c) -> (e g) c", c=512))
        load_direct(0, 0)
        load_w2(0, 0)
        load_w2(0, 1)
        x_all = const.tile([P, E, D], BF16, name="x_all", align_bytes=64)
        x_src = x.rearrange("(e p) d -> p e d", p=P)
        nc.sync.dma_start(out=x_all[:, 0:2, :], in_=x_src[:, 0:2, :])
        temp = const.tile([P, 1], BF16, name="temp", align_bytes=64)
        nc.sync.dma_start(out=temp[:], in_=temperature.partition_broadcast(P))
        for g in range(1, G):
            load_direct(0, g)
        load_w2(1, 0)
        load_direct(1, 0)

        ident = const.tile([P, P], F32, name="ident", align_bytes=64)
        make_identity(nc, ident[:])

        nc.vector.tensor_copy(out=rows[0:32, :], in_=b1_rows[:])
        rows_s = out_pool.tile([P, 4, P], F32, name="rows_s", tag="bg", align_bytes=64)
        nc.vector.tensor_copy(out=rows_s[:], in_=rows[:].rearrange("r (m s) -> r s m", s=4))
        col_ps = ps_t.tile([P, 4, P], F32, name="tp")
        for s in range(4):
            nc.tensor.transpose(col_ps[:, s, :], rows_s[:, s, :], ident[:])
        cols = const.tile([P, 36, 4], F32, name="cols", align_bytes=64)
        nc.vector.tensor_copy(out=cols[:], in_=col_ps[:, :, 0:36].rearrange("p s r -> p r s"))

        xq = const.tile([P, E, TOK], U32, name="xq", align_bytes=64)
        xs = const.tile([P, E, TOK], U8, name="xs", align_bytes=64)
        xg_t, gain = {}, const.tile([P, 1], F32, name="gain", align_bytes=64)

        def gain_calc():
            clamped = const.tile([P, 1], F32, name="clamped", align_bytes=64)
            nc.vector.tensor_scalar_min(clamped[:], temp[:], CLAMP_MAX)
            nc.scalar.activation(out=gain[:], in_=clamped[:], func=ACT.Exp)

        def x_turn(k):
            tp = ps_t.tile([P, 4, P], F32, name="tp")
            for i in range(2):
                words = x_all[:, 2 * k + i, :].bitcast(F32)
                for u in range(2):
                    nc.tensor.transpose(tp[:, 2 * i + u, :], words[:, u:256:2], ident[:])
            xg = work.tile([P, 2, TOK, 4], BF16, name="xg", align_bytes=64, bufs=1)
            for i in range(2):
                copy("s", xg[:, i, :, :].bitcast(F32), tp[:, 2 * i:2 * i + 2, :].rearrange("p u r -> p r u"))
            xg_t[k] = xg

        def x_quantise(k):
            nc.vector.quantize_mx(
                out=xq[:, 2 * k:2 * k + 2, :].rearrange("p e r -> p (e r)").bitcast(FP8X4),
                scales=xs[:, 2 * k:2 * k + 2, :].rearrange("p e r -> p (e r)"),
                in_=xg_t[k][:].rearrange("p e r t -> p (e r t)"),
            )

        w1_grp, w1_cod, w2_pl, w2_grp, w2_cod, h_ps, h_pl, h_grp, h_cod, y_ps, b2g = ({} for i in range(11))

        def direct_interleave(e, g):
            grp = grp_pool.tile([P, 4, P, 4], BF16, name="w1g", align_bytes=64)
            src = w1_raw[e, g][:].rearrange("p j (m s) -> p m s j", s=4)
            dst = grp[:].rearrange("p s m j -> p m s j")
            if D_ENG[(G * e + g) % len(D_ENG)] == "v":
                nc.vector.tensor_copy(out=dst, in_=src)
            else:
                nc.scalar.copy(out=dst, in_=src)
            w1_grp[e, g] = grp

        def direct_quantise(e, g):
            q = grp_pool.tile([P, 512], U32, name="w1q", align_bytes=64)
            sc = grp_pool.tile([P, 512], U8, name="w1s", align_bytes=64)
            nc.vector.quantize_mx(
                out=q[:].bitcast(FP8X4), scales=sc[:],
                in_=w1_grp[e, g][:].rearrange("p s m j -> p (s m j)"),
            )
            w1_cod[e, g] = (q, sc)

        def direct_mm1(e, g):
            q, sc = w1_cod[e, g]
            ph = ps_h.tile([P, 4, TOK], F32, name="ph")
            for s in range(4):
                nc.tensor.matmul_mx(
                    out=ph[:, s, :],
                    lhsT=q[:, s * P:(s + 1) * P].bitcast(FP8X4), lhsT_scale=sc[:, s * P:(s + 1) * P],
                    rhs=xq[:, e, :].bitcast(FP8X4), rhs_scale=xs[:, e, :],
                    start=True, stop=True,
                )
            for s in range(4):
                h_ps[e, g, s] = ph[:, s, :]

        def h_relu(e, g, s):
            if e not in h_pl:
                h_pl[e] = work.tile([P, 4, G * TOK], BF16, name="hp", align_bytes=64, bufs=4)
            nc.scalar.activation(
                out=h_pl[e][:, s, g * TOK:(g + 1) * TOK], in_=h_ps[e, g, s],
                func=ACT.Relu, bias=cols[:, 4 * e + g, s:s + 1],
            )

        def h_interleave(e):
            grp = work.tile([P, G * TOK, 4], BF16, name="hg", align_bytes=64, bufs=2)
            split_copy(
                grp[:].rearrange("p (c i) s -> p c s i", i=4),
                h_pl[e][:].rearrange("p s (c i) -> p c s i", i=4),
                64 if e >= 6 else H_SPLIT,
            )
            h_grp[e] = grp

        def h_quantise(e):
            q = hq_pool.tile([P, G * TOK], U32, name="hq", align_bytes=64)
            sc = hq_pool.tile([P, G * TOK], U8, name="hs", align_bytes=64)
            nc.vector.quantize_mx(
                out=q[:].bitcast(FP8X4), scales=sc[:], in_=h_grp[e][:].rearrange("p n s -> p (n s)")
            )
            h_cod[e] = (q, sc)

        def w2_widen(e, g):
            plane = work.tile([P, 2, 512, 2], BF16, name="w2p", align_bytes=64, bufs=3)
            for s in (0, 2, 1, 3):
                nc.vector.tensor_scalar(
                    out=plane[:, s // 2, :, s % 2],
                    in0=w2_raw[e, g // 2][:, g % 2, s * 512:(s + 1) * 512].bitcast(FP8),
                    scalar1=cols[:, 32 + g, s:s + 1], scalar2=None, op0=ALU.mult,
                )
            w2_pl[e, g] = plane

        def w2_interleave(e, g):
            grp = work.tile([P, 512, 4], BF16, name="w2g", align_bytes=64, bufs=4)
            nc.scalar.copy(
                out=grp[:].bitcast(F32),
                in_=w2_pl[e, g][:].rearrange("p h n l -> p h (n l)").bitcast(F32).rearrange("p h n -> p n h"),
            )
            w2_grp[e, g] = grp

        def w2_quantise(e, g):
            q = w2_codes.tile([P, 512], U32, name="w2q", align_bytes=64)
            sc = w2_codes.tile([P, 512], U8, name="w2s", align_bytes=64)
            nc.vector.quantize_mx(
                out=q[:].bitcast(FP8X4), scales=sc[:], in_=w2_grp[e, g][:].rearrange("p n s -> p (n s)")
            )
            w2_cod[e, g] = (q, sc)

        def mm2(e):
            py = ps_y.tile([TOK, D], F32, name="py")
            hq, hs = h_cod[e]
            for g in range(G):
                wq, ws = w2_cod[e, g]
                c = slice(g * TOK, (g + 1) * TOK)
                nc.tensor.matmul_mx(
                    out=py[:], lhsT=hq[:, c].bitcast(FP8X4), lhsT_scale=hs[:, c],
                    rhs=wq[:].bitcast(FP8X4), rhs_scale=ws[:],
                    start=(g == 0), stop=(g == G - 1),
                )
            y_ps[e] = py

        def b2_load(experts):
            for e in experts:
                b2_tile[e] = out_pool.tile([P, D], BF16, name="b2_row", align_bytes=64, bufs=4)
                nc.sync.dma_start(out=b2_tile[e][:], in_=b2[e, :].partition_broadcast(P))

        def bias2(e):
            bg = out_pool.tile([P, D], F32, name="bg", align_bytes=64)
            nc.vector.tensor_scalar(
                out=bg[:], in0=b2_tile[e][:], scalar1=gain[:], scalar2=None, op0=ALU.mult
            )
            b2g[e] = bg

        def store(e):
            y = out_pool.tile([TOK, D], F32, name="y", align_bytes=64)
            nc.vector.scalar_tensor_tensor(
                out=y[:], in0=y_ps[e][:], scalar=gain[:], in1=b2g[e][:], op0=ALU.mult, op1=ALU.add
            )
            nc.sync.dma_start(out=out[e * TOK:(e + 1) * TOK, :], in_=y[:])

        h_jobs = {}

        def finish(n, experts):
            for j, e in enumerate(experts):
                h_jobs.setdefault(n + 1 + j, []).append(lambda e=e: h_interleave(e))
                h_jobs.setdefault(n + 2 + j, []).append(lambda e=e: h_output(e))
                h_jobs.setdefault(n + 3 + j, []).insert(0, lambda e=e: store(e))

        def h_output(e):
            h_quantise(e)
            bias2(e)
            mm2(e)

        def h_beat(n):
            for job in h_jobs.pop(n, []):
                job()

        units = [(e, g) for e in range(E) for g in range(G)]
        n_units = len(units)

        def late(n, lag):
            return units[n - lag] if 0 <= n - lag < n_units else None

        for n in range(n_units + RELU_LAG + 4):
            u = late(n, 0)
            if u:
                w2_widen(*u)
            if n == 1:
                x_quantise(0)
            v = late(n, Q_LAG)
            if v:
                direct_quantise(*v)
                direct_mm1(*v)
            v = late(n, W_LAG)
            if v:
                w2_quantise(*v)
            v = late(n, RELU_LAG)
            if v:
                for s in range(4):
                    h_relu(*v, s)
                if v[1] == G - 1:
                    finish(n, [v[0]])
            h_beat(n)
            if u:
                direct_interleave(*u)
                if n == 0:
                    x_turn(0)
                w2_interleave(*u)
                e, g = u
                if e in (1, 2, 3) and g == 0:
                    x_turn(e)
                if e in (1, 2, 3) and g == 1:
                    x_quantise(e)
                if n == 3:
                    gain_calc()
                if n + 5 < n_units:
                    load_direct(*units[n + 5])
                if g % 2 == 1 and n + 5 < n_units:
                    load_w2(units[n + 5][0], units[n + 5][1] // 2)
                if g == 0:
                    b2_load((e,))
                if n == 1:
                    nc.sync.dma_start(out=x_all[:, 2:8, :], in_=x_src[:, 2:8, :])
